import numpy as np
import ml_dtypes

BF16 = ml_dtypes.bfloat16


def bf(x):
    return np.asarray(x, np.float32).astype(BF16)


def f32(x):
    return np.asarray(x, np.float32)


def f64(x):
    return np.asarray(x).astype(np.float64)


def striped(idx):
    return np.tile(idx.reshape(-1, 16).T, (8, 1))


C, S, N, T, F, K = 128, 512, 128, 256, 4, 32
SHARP = 3.0


def setup_inputs():
    logits = SHARP * np.random.standard_normal((T, F, K))
    soft = np.exp(logits - logits.max(axis=-1, keepdims=True))
    soft = soft / soft.sum(axis=-1, keepdims=True)
    return {"base": f32(np.random.uniform(size=(C, S))), "teacher": bf(np.random.uniform(size=(T, C))), "membership": bf(soft.reshape(T, N)), "offs": striped(np.random.permutation(S)[:N])}


def reference(base, teacher, membership, offs):
    idx = offs[:16].T.reshape(-1)
    sw = f64(teacher).T @ f64(membership)
    mass = f64(membership).sum(axis=0, keepdims=True)
    out = f64(base).copy()
    out[:, idx] = sw * (1.0 / mass)
    return out

@@ -1,0 +1,45 @@
+import concourse.mybir as mybir
+
+C, S, N, T = 128, 512, 128, 256
+P = 128
+TB = T // P
+FLOPS = 2 * T * C * N + T * N + C * N
+
+BF16, F32, U16 = mybir.dt.bfloat16, mybir.dt.float32, mybir.dt.uint16
+MULT = mybir.AluOpType.mult
+
+
+def tile_dispersionloss_kernel(tc, base, teacher, membership, offs, out):
+    nc = tc.nc
+    with (
+        tc.tile_pool(name="held", bufs=1) as held,
+        tc.psum_pool(name="psum", bufs=1) as psum,
+    ):
+        member_sb = held.tile([P, TB, N], BF16, name="member_sb")
+        nc.scalar.dma_start(member_sb[:], membership.rearrange("(p b) j -> p b j", b=TB))
+        teacher_sb = held.tile([P, TB, C], BF16, name="teacher_sb")
+        nc.scalar.dma_start(teacher_sb[:], teacher.rearrange("(p b) c -> p b c", b=TB))
+        window = held.tile([C, S], F32, name="window")
+        nc.sync.dma_start(window[:], base)
+        offsets = held.tile([P, N // 16], U16, name="offsets")
+        nc.sync.dma_start(offsets[:], offs)
+
+        ones = held.tile([P, C], BF16, name="ones")
+        nc.vector.memset(ones[:], 1.0)
+
+        mass_ps = psum.tile([C, N], F32, name="mass_ps")
+        for b in range(TB):
+            nc.tensor.matmul(mass_ps[:], ones[:], member_sb[:, b, :], start=(b == 0), stop=(b == TB - 1))
+        sw_ps = psum.tile([C, N], F32, name="sw_ps")
+        for b in range(TB):
+            nc.tensor.matmul(sw_ps[:], teacher_sb[:, b, :], member_sb[:, b, :], start=(b == 0), stop=(b == TB - 1))
+
+        inv_mass = held.tile([C, N], F32, name="inv_mass")
+        nc.vector.reciprocal(inv_mass[:], mass_ps[:])
+
+        sw_sb = held.tile([C, N], F32, name="sw_sb")
+        nc.scalar.copy(sw_sb[:], sw_ps[:])
+
+        nc.vector.tensor_tensor(window[:].indirect(offsets[:]), sw_sb[:], inv_mass[:], MULT)
+
+        nc.sync.dma_start(out, window[:])

@@ -3,6 +3,7 @@ import concourse.mybir as mybir
 C, S, N, T = 128, 512, 128, 256
 P = 128
 TB = T // P
+H = S // 2
 FLOPS = 2 * T * C * N + T * N + C * N
 
 BF16, F32, U16 = mybir.dt.bfloat16, mybir.dt.float32, mybir.dt.uint16
@@ -16,11 +17,12 @@ def tile_dispersionloss_kernel(tc, base, teacher, membership, offs, out):
         tc.psum_pool(name="psum", bufs=1) as psum,
     ):
         member_sb = held.tile([P, TB, N], BF16, name="member_sb")
-        nc.scalar.dma_start(member_sb[:], membership.rearrange("(p b) j -> p b j", b=TB))
+        nc.sync.dma_start(member_sb[:], membership.rearrange("(p b) j -> p b j", b=TB))
         teacher_sb = held.tile([P, TB, C], BF16, name="teacher_sb")
         nc.scalar.dma_start(teacher_sb[:], teacher.rearrange("(p b) c -> p b c", b=TB))
         window = held.tile([C, S], F32, name="window")
-        nc.sync.dma_start(window[:], base)
+        nc.sync.dma_start(window[:, 0:H], base[:, 0:H])
+        nc.scalar.dma_start(window[:, H:S], base[:, H:S])
         offsets = held.tile([P, N // 16], U16, name="offsets")
         nc.sync.dma_start(offsets[:], offs)
 
@@ -42,4 +44,5 @@ def tile_dispersionloss_kernel(tc, base, teacher, membership, offs, out):
 
         nc.vector.tensor_tensor(window[:].indirect(offsets[:]), sw_sb[:], inv_mass[:], MULT)
 
-        nc.sync.dma_start(out, window[:])
+        nc.sync.dma_start(out[:, 0:H], window[:, 0:H])
+        nc.scalar.dma_start(out[:, H:S], window[:, H:S])

@@ -3,7 +3,8 @@ import concourse.mybir as mybir
 C, S, N, T = 128, 512, 128, 256
 P = 128
 TB = T // P
-H = S // 2
+Q = 4
+W = S // Q
 FLOPS = 2 * T * C * N + T * N + C * N
 
 BF16, F32, U16 = mybir.dt.bfloat16, mybir.dt.float32, mybir.dt.uint16
@@ -12,6 +13,7 @@ MULT = mybir.AluOpType.mult
 
 def tile_dispersionloss_kernel(tc, base, teacher, membership, offs, out):
     nc = tc.nc
+    queues = (nc.sync, nc.scalar)
     with (
         tc.tile_pool(name="held", bufs=1) as held,
         tc.psum_pool(name="psum", bufs=1) as psum,
@@ -21,8 +23,8 @@ def tile_dispersionloss_kernel(tc, base, teacher, membership, offs, out):
         teacher_sb = held.tile([P, TB, C], BF16, name="teacher_sb")
         nc.scalar.dma_start(teacher_sb[:], teacher.rearrange("(p b) c -> p b c", b=TB))
         window = held.tile([C, S], F32, name="window")
-        nc.sync.dma_start(window[:, 0:H], base[:, 0:H])
-        nc.scalar.dma_start(window[:, H:S], base[:, H:S])
+        for q in range(Q):
+            queues[q % 2].dma_start(window[:, q * W : (q + 1) * W], base[:, q * W : (q + 1) * W])
         offsets = held.tile([P, N // 16], U16, name="offsets")
         nc.sync.dma_start(offsets[:], offs)
 
@@ -44,5 +46,5 @@ def tile_dispersionloss_kernel(tc, base, teacher, membership, offs, out):
 
         nc.vector.tensor_tensor(window[:].indirect(offsets[:]), sw_sb[:], inv_mass[:], MULT)
 
-        nc.sync.dma_start(out[:, 0:H], window[:, 0:H])
-        nc.scalar.dma_start(out[:, H:S], window[:, H:S])
+        for q in range(Q):
+            queues[q % 2].dma_start(out[:, q * W : (q + 1) * W], window[:, q * W : (q + 1) * W])

@@ -3,8 +3,6 @@ import concourse.mybir as mybir
 C, S, N, T = 128, 512, 128, 256
 P = 128
 TB = T // P
-Q = 4
-W = S // Q
 FLOPS = 2 * T * C * N + T * N + C * N
 
 BF16, F32, U16 = mybir.dt.bfloat16, mybir.dt.float32, mybir.dt.uint16
@@ -13,7 +11,6 @@ MULT = mybir.AluOpType.mult
 
 def tile_dispersionloss_kernel(tc, base, teacher, membership, offs, out):
     nc = tc.nc
-    queues = (nc.sync, nc.scalar)
     with (
         tc.tile_pool(name="held", bufs=1) as held,
         tc.psum_pool(name="psum", bufs=1) as psum,
@@ -23,8 +20,7 @@ def tile_dispersionloss_kernel(tc, base, teacher, membership, offs, out):
         teacher_sb = held.tile([P, TB, C], BF16, name="teacher_sb")
         nc.scalar.dma_start(teacher_sb[:], teacher.rearrange("(p b) c -> p b c", b=TB))
         window = held.tile([C, S], F32, name="window")
-        for q in range(Q):
-            queues[q % 2].dma_start(window[:, q * W : (q + 1) * W], base[:, q * W : (q + 1) * W])
+        nc.scalar.dma_start(window[:], base)
         offsets = held.tile([P, N // 16], U16, name="offsets")
         nc.sync.dma_start(offsets[:], offs)
 
@@ -46,5 +42,4 @@ def tile_dispersionloss_kernel(tc, base, teacher, membership, offs, out):
 
         nc.vector.tensor_tensor(window[:].indirect(offsets[:]), sw_sb[:], inv_mass[:], MULT)
 
-        for q in range(Q):
-            queues[q % 2].dma_start(out[:, q * W : (q + 1) * W], window[:, q * W : (q + 1) * W])
+        nc.sync.dma_start(out, window[:])

@@ -18,7 +18,7 @@ def tile_dispersionloss_kernel(tc, base, teacher, membership, offs, out):
         member_sb = held.tile([P, TB, N], BF16, name="member_sb")
         nc.sync.dma_start(member_sb[:], membership.rearrange("(p b) j -> p b j", b=TB))
         teacher_sb = held.tile([P, TB, C], BF16, name="teacher_sb")
-        nc.scalar.dma_start(teacher_sb[:], teacher.rearrange("(p b) c -> p b c", b=TB))
+        nc.sync.dma_start(teacher_sb[:], teacher.rearrange("(p b) c -> p b c", b=TB))
         window = held.tile([C, S], F32, name="window")
         nc.scalar.dma_start(window[:], base)
         offsets = held.tile([P, N // 16], U16, name="offsets")

@@ -38,7 +38,7 @@ def tile_dispersionloss_kernel(tc, base, teacher, membership, offs, out):
         nc.vector.reciprocal(inv_mass[:], mass_ps[:])
 
         sw_sb = held.tile([C, N], F32, name="sw_sb")
-        nc.scalar.copy(sw_sb[:], sw_ps[:])
+        nc.vector.tensor_copy(sw_sb[:], sw_ps[:])
 
         nc.vector.tensor_tensor(window[:].indirect(offsets[:]), sw_sb[:], inv_mass[:], MULT)
 

@@ -3,6 +3,7 @@ import concourse.mybir as mybir
 C, S, N, T = 128, 512, 128, 256
 P = 128
 TB = T // P
+PIECES = ((0, 32), (32, N))
 FLOPS = 2 * T * C * N + T * N + C * N
 
 BF16, F32, U16 = mybir.dt.bfloat16, mybir.dt.float32, mybir.dt.uint16
@@ -27,15 +28,17 @@ def tile_dispersionloss_kernel(tc, base, teacher, membership, offs, out):
         ones = held.tile([P, C], BF16, name="ones")
         nc.vector.memset(ones[:], 1.0)
 
-        mass_ps = psum.tile([C, N], F32, name="mass_ps")
-        for b in range(TB):
-            nc.tensor.matmul(mass_ps[:], ones[:], member_sb[:, b, :], start=(b == 0), stop=(b == TB - 1))
+        mass_ps = [psum.tile([C, hi - lo], F32, name="mass_ps%d" % lo) for lo, hi in PIECES]
+        for piece_ps, (lo, hi) in zip(mass_ps, PIECES):
+            for b in range(TB):
+                nc.tensor.matmul(piece_ps[:], ones[:], member_sb[:, b, lo:hi], start=(b == 0), stop=(b == TB - 1))
         sw_ps = psum.tile([C, N], F32, name="sw_ps")
         for b in range(TB):
             nc.tensor.matmul(sw_ps[:], teacher_sb[:, b, :], member_sb[:, b, :], start=(b == 0), stop=(b == TB - 1))
 
         inv_mass = held.tile([C, N], F32, name="inv_mass")
-        nc.vector.reciprocal(inv_mass[:], mass_ps[:])
+        for piece_ps, (lo, hi) in zip(mass_ps, PIECES):
+            nc.vector.reciprocal(inv_mass[:, lo:hi], piece_ps[:])
 
         sw_sb = held.tile([C, N], F32, name="sw_sb")
         nc.vector.tensor_copy(sw_sb[:], sw_ps[:])

@@ -21,7 +21,7 @@ def tile_dispersionloss_kernel(tc, base, teacher, membership, offs, out):
         teacher_sb = held.tile([P, TB, C], BF16, name="teacher_sb")
         nc.sync.dma_start(teacher_sb[:], teacher.rearrange("(p b) c -> p b c", b=TB))
         window = held.tile([C, S], F32, name="window")
-        nc.scalar.dma_start(window[:], base)
+        nc.sync.dma_start(window[:], base)
         offsets = held.tile([P, N // 16], U16, name="offsets")
         nc.sync.dma_start(offsets[:], offs)
 

@@ -19,7 +19,7 @@ def tile_dispersionloss_kernel(tc, base, teacher, membership, offs, out):
         member_sb = held.tile([P, TB, N], BF16, name="member_sb")
         nc.sync.dma_start(member_sb[:], membership.rearrange("(p b) j -> p b j", b=TB))
         teacher_sb = held.tile([P, TB, C], BF16, name="teacher_sb")
-        nc.sync.dma_start(teacher_sb[:], teacher.rearrange("(p b) c -> p b c", b=TB))
+        nc.scalar.dma_start(teacher_sb[:], teacher.rearrange("(p b) c -> p b c", b=TB))
         window = held.tile([C, S], F32, name="window")
         nc.sync.dma_start(window[:], base)
         offsets = held.tile([P, N // 16], U16, name="offsets")

@@ -21,7 +21,8 @@ def tile_dispersionloss_kernel(tc, base, teacher, membership, offs, out):
         teacher_sb = held.tile([P, TB, C], BF16, name="teacher_sb")
         nc.scalar.dma_start(teacher_sb[:], teacher.rearrange("(p b) c -> p b c", b=TB))
         window = held.tile([C, S], F32, name="window")
-        nc.sync.dma_start(window[:], base)
+        nc.sync.dma_start(window[:, 0 : S // 2], base[:, 0 : S // 2])
+        nc.scalar.dma_start(window[:, S // 2 : S], base[:, S // 2 : S])
         offsets = held.tile([P, N // 16], U16, name="offsets")
         nc.sync.dma_start(offsets[:], offs)
 

import concourse.mybir as mybir

C, S, N, T = 128, 512, 128, 256
P = 128
TB = T // P
PIECES = ((0, 32), (32, N))
FLOPS = 2 * T * C * N + T * N + C * N

BF16, F32, U16 = mybir.dt.bfloat16, mybir.dt.float32, mybir.dt.uint16
MULT = mybir.AluOpType.mult


def tile_dispersionloss_kernel(tc, base, teacher, membership, offs, out):
    nc = tc.nc
    with (
        tc.tile_pool(name="held", bufs=1) as held,
        tc.psum_pool(name="psum", bufs=1) as psum,
    ):
        member_sb = held.tile([P, TB, N], BF16, name="member_sb")
        nc.sync.dma_start(member_sb[:], membership.rearrange("(p b) j -> p b j", b=TB))
        teacher_sb = held.tile([P, TB, C], BF16, name="teacher_sb")
        nc.scalar.dma_start(teacher_sb[:], teacher.rearrange("(p b) c -> p b c", b=TB))
        window = held.tile([C, S], F32, name="window")
        nc.sync.dma_start(window[:, 0 : S // 2], base[:, 0 : S // 2])
        nc.scalar.dma_start(window[:, S // 2 : S], base[:, S // 2 : S])
        offsets = held.tile([P, N // 16], U16, name="offsets")
        nc.sync.dma_start(offsets[:], offs)

        ones = held.tile([P, C], BF16, name="ones")
        nc.vector.memset(ones[:], 1.0)

        mass_ps = [psum.tile([C, hi - lo], F32, name="mass_ps%d" % lo) for lo, hi in PIECES]
        for piece_ps, (lo, hi) in zip(mass_ps, PIECES):
            for b in range(TB):
                nc.tensor.matmul(piece_ps[:], ones[:], member_sb[:, b, lo:hi], start=(b == 0), stop=(b == TB - 1))
        sw_ps = psum.tile([C, N], F32, name="sw_ps")
        for b in range(TB):
            nc.tensor.matmul(sw_ps[:], teacher_sb[:, b, :], member_sb[:, b, :], start=(b == 0), stop=(b == TB - 1))

        inv_mass = held.tile([C, N], F32, name="inv_mass")
        for piece_ps, (lo, hi) in zip(mass_ps, PIECES):
            nc.vector.reciprocal(inv_mass[:, lo:hi], piece_ps[:])

        sw_sb = held.tile([C, N], F32, name="sw_sb")
        nc.vector.tensor_copy(sw_sb[:], sw_ps[:])

        nc.vector.tensor_tensor(window[:].indirect(offsets[:]), sw_sb[:], inv_mass[:], MULT)

        nc.sync.dma_start(out, window[:])
